import numpy as np
import ml_dtypes


def mxq(x, axis, fmt="e4m3"):
    dtype, down = {"e4m3": (ml_dtypes.float8_e4m3fn, 7), "e5m2": (ml_dtypes.float8_e5m2, 14)}[fmt]
    v = np.moveaxis(np.asarray(x, np.float32).astype(ml_dtypes.bfloat16).astype(np.float64), axis, -1)
    blocks = v.reshape(v.shape[:-1] + (-1, 32))
    amax = np.abs(blocks).max(-1, keepdims=True)
    byte = np.maximum(np.where(amax > 0, np.frexp(amax)[1] - 1 + 127, 0) - down, 1)
    scale = np.exp2(byte - 127.0)
    codes = (blocks / scale).astype(np.float32).astype(dtype).astype(np.float64)
    return np.moveaxis((codes * scale).reshape(v.shape), -1, axis)


WIDE = False


def mx_kscale(k):
    if not WIDE:
        return np.ones(k)
    levels = np.array([10, -10, 5, -5, 0])
    a = np.random.permutation(np.resize(levels, k // 512 * 4)).reshape(k // 512, 4)
    idx = np.arange(k)
    return np.exp2(a[idx // 512, idx % 128 // 32])


BF16 = ml_dtypes.bfloat16


def bf(x):
    return np.asarray(x, np.float32).astype(BF16)


def f64(x):
    return np.asarray(x).astype(np.float64)


E2M1 = np.array([0.0, 0.5, 1.0, 1.5, 2.0, 3.0, 4.0, 6.0, -0.0, -0.5, -1.0, -1.5, -2.0, -3.0, -4.0, -6.0])


def pack_weight(w, fmt):
    k, n = w.shape
    w = f64(bf(w)).reshape(k // 32, 32, n)
    amax = np.abs(w).max(1)
    if fmt == "e4m3":
        byte = np.frexp(amax)[1] - 1 + 127 - 7
    else:
        mant, ex = np.frexp(amax / 6.0)
        byte = np.where(mant > 0.5, ex, ex - 1) + 127
    byte = np.clip(np.where(amax > 0, byte, 1), 1, 254)
    scaled = (w * np.exp2(127.0 - byte)[:, None, :]).reshape(k, n).astype(np.float32)
    by_word = np.ascontiguousarray(scaled.reshape(k // 512, 128, 4, n).transpose(0, 1, 3, 2))
    if fmt == "e4m3":
        words = by_word.astype(ml_dtypes.float8_e4m3fn).view(np.uint8)
    else:
        c = by_word.astype(ml_dtypes.float4_e2m1fn).view(np.uint8) & 0xF
        words = c[..., 0::2] | (c[..., 1::2] << 4)
    return np.ascontiguousarray(words), np.ascontiguousarray(byte.astype(np.uint8).reshape(k // 512, 16, n))


def unpack_weight(words, scales, fmt):
    g, p, n, _ = words.shape
    if fmt == "e4m3":
        vals = np.ascontiguousarray(words).view(ml_dtypes.float8_e4m3fn).astype(np.float64)
    else:
        nib = np.empty((g, p, n, 4), np.uint8)
        nib[..., 0::2] = words & 0xF
        nib[..., 1::2] = words >> 4
        vals = E2M1[nib]
    vals = vals * np.repeat(np.exp2(scales.astype(np.float64) - 127.0), 8, axis=1)[..., None]
    return vals.transpose(0, 1, 3, 2).reshape(g * 512, n)


S, M, L1, L2, L3, B, NG = 512, 512, 1024, 1024, 1024, 256, 4
FMT = "e4m3"


def sigmoid(v):
    return 1.0 / (1.0 + np.exp(-v))


def lstm_cell(x, h, c, Wih_t, Whh_t, bih, bhh):
    g = (mxq(x, 1, "e4m3") @ Wih_t) + (mxq(h, 1, "e4m3") @ Whh_t) + (bih + bhh)
    i, f, gg, o = np.split(g, NG, axis=-1)
    c_new = sigmoid(f) * c + sigmoid(i) * np.tanh(gg)
    h_new = sigmoid(o) * np.tanh(c_new)
    return h_new, c_new


def log_softmax(v):
    shifted = v - v.max(-1, keepdims=True)
    return shifted - np.log(np.exp(shifted).sum(-1, keepdims=True))


def setup_inputs():
    rn = np.random.standard_normal
    s, t2, t3 = mx_kscale(S), mx_kscale(L2), mx_kscale(L3)
    x = bf(rn((B, S)) * s)
    y2 = bf(rn((B, L2)) * 0.3 * t2)
    h3 = bf(rn((B, L3)) * t3)
    c3 = bf(rn((B, L3)))
    Wih3_words, Wih3_scales = pack_weight(np.ascontiguousarray((rn((NG * L3, L2)) * 2.0 / np.sqrt(L2) / t2).T), FMT)
    Whh3_words, Whh3_scales = pack_weight(np.ascontiguousarray((rn((NG * L3, L3)) * 0.7 / np.sqrt(L3) / t3).T), FMT)
    bih3 = bf(rn(NG * L3) * 0.3)
    bhh3 = bf(rn(NG * L3) * 0.3)
    Wd_words, Wd_scales = pack_weight(np.ascontiguousarray((rn((L3, S)) * 0.5 / np.sqrt(S) / s).T), FMT)
    bd = bf(rn(L3) * 0.2)
    Wm_words, Wm_scales = pack_weight(np.ascontiguousarray((rn((M, L3)) * 3.0 / np.sqrt(L3)).T), FMT)
    bm = bf(rn(M) * 0.5)
    return {
        "x": x,
        "y2": y2,
        "h3": h3, "c3": c3,
        "Wih3_words": Wih3_words, "Wih3_scales": Wih3_scales,
        "Whh3_words": Whh3_words, "Whh3_scales": Whh3_scales,
        "bih3": bih3, "bhh3": bhh3,
        "Wd_words": Wd_words, "Wd_scales": Wd_scales, "bd": bd,
        "Wm_words": Wm_words, "Wm_scales": Wm_scales, "bm": bm,
    }


def reference(x, y2, h3, c3, Wih3_words, Wih3_scales, Whh3_words, Whh3_scales, bih3, bhh3, Wd_words, Wd_scales, bd, Wm_words, Wm_scales, bm):
    y3, nc3 = lstm_cell(f64(y2), f64(h3), f64(c3), unpack_weight(Wih3_words, Wih3_scales, FMT), unpack_weight(Whh3_words, Whh3_scales, FMT), f64(bih3), f64(bhh3))
    mid = (mxq(f64(x), 1, "e4m3") @ unpack_weight(Wd_words, Wd_scales, FMT)) + f64(bd) + y3
    motors = (mxq(mid, 1, "e4m3") @ unpack_weight(Wm_words, Wm_scales, FMT)) + f64(bm)
    return log_softmax(motors), y3, nc3

@@ -1,0 +1,304 @@
+from contextlib import ExitStack
+
+import concourse.mybir as mybir
+from concourse.masks import make_identity
+
+F32 = mybir.dt.float32
+BF16 = mybir.dt.bfloat16
+I32 = mybir.dt.int32
+U32 = mybir.dt.uint32
+U8 = mybir.dt.uint8
+FP8X4 = mybir.dt.float8_e4m3fn_x4
+ALU = mybir.AluOpType
+ACT = mybir.ActivationFunctionType
+AXIS = mybir.AxisListType
+
+P = 128
+PACK = 4
+K_PASS = P * PACK
+N_TILE = 512
+QUADS = 4
+
+BATCH = 256
+BT = BATCH // P
+S_IN = 512
+HID = 1024
+MOTORS = 512
+HALVES = HID // N_TILE
+GATE_I, GATE_F, GATE_G, GATE_O = 0, 1, 2, 3
+GATE_ORDER = (GATE_F, GATE_I, GATE_G, GATE_O)
+GATE_COLS = 4 * HID
+BIAS_COLS = GATE_COLS + HID + MOTORS
+
+FLOPS = 2 * BATCH * (2 * HID * GATE_COLS + S_IN * HID + HID * MOTORS)
+
+
+def packed_words(words):
+    return words.rearrange("g p n t -> p g (n t)").bitcast(I32)
+
+
+def tile_network_pb_kernel(
+    tc, x, y2, h3, c3,
+    Wih3_words, Wih3_scales, Whh3_words, Whh3_scales, bih3, bhh3,
+    Wd_words, Wd_scales, bd, Wm_words, Wm_scales, bm,
+    out_0, out_1, out_2,
+):
+    nc = tc.nc
+    with ExitStack() as stack:
+        keep = stack.enter_context(tc.tile_pool(name="keep", bufs=1))
+        acc_pool = stack.enter_context(tc.psum_pool(name="acc", bufs=6))
+        plain_pool = stack.enter_context(tc.psum_pool(name="plain", bufs=2))
+        stack.enter_context(tc.manual_schedule())
+
+        gate_planes = keep.tile([P, GATE_COLS], U8, name="gate_planes", align_bytes=64)
+        side_planes = keep.tile([P, HID], U8, name="side_planes", align_bytes=64)
+        nc.vector.memset(gate_planes[:].bitcast(I32), 0)
+        nc.vector.memset(side_planes[:].bitcast(I32), 0)
+        bias_rows = keep.tile([P, BIAS_COLS], BF16, name="bias_rows")
+        nc.vector.memset(bias_rows[:].bitcast(I32), 0)
+        zero_col = keep.tile([P, 1], F32, name="zero_col")
+        nc.vector.memset(zero_col[:], 0.0)
+
+        ident_f32 = keep.tile([P, P], F32, name="ident_f32")
+        make_identity(nc, ident_f32[:])
+        ident_bf16 = keep.tile([P, P], BF16, name="ident_bf16")
+        make_identity(nc, ident_bf16[:])
+        ones = keep.tile([P, P], BF16, name="ones")
+        nc.gpsimd.memset(ones[:], 1.0)
+
+        nc.scalar.dma_start(out=bias_rows[0:1, 0:GATE_COLS], in_=bih3.rearrange("(o n) -> o n", o=1))
+        nc.scalar.dma_start(out=bias_rows[1:2, 0:GATE_COLS], in_=bhh3.rearrange("(o n) -> o n", o=1))
+        nc.scalar.dma_start(
+            out=bias_rows[0:1, GATE_COLS : GATE_COLS + HID], in_=bd.rearrange("(o n) -> o n", o=1)
+        )
+        nc.scalar.dma_start(
+            out=bias_rows[0:1, GATE_COLS + HID : BIAS_COLS], in_=bm.rearrange("(o n) -> o n", o=1)
+        )
+        table_warm = keep.tile([P, 1], F32, name="table_warm")
+        nc.scalar.activation(out=table_warm[:], in_=zero_col[:], func=ACT.Sigmoid)
+
+        def load_rows(src, width, name):
+            rows = keep.tile([P, BT, width], BF16, name=name)
+            nc.sync.dma_start(out=rows[:], in_=src.rearrange("(bt p) k -> p bt k", p=P))
+            return rows
+
+        y2_rows = load_rows(y2, HID, "y2_rows")
+        h3_rows = load_rows(h3, HID, "h3_rows")
+
+        for quad in range(QUADS):
+            rows4 = slice(4 * quad, 4 * quad + 4)
+            for w, scales in enumerate((Wih3_scales, Whh3_scales)):
+                first = 32 * quad + 8 * w
+                nc.sync.dma_start(
+                    out=gate_planes[first : first + 8, :].bitcast(I32),
+                    in_=scales[:, rows4, :].bitcast(I32),
+                )
+        for quad in range(QUADS):
+            rows4 = slice(4 * quad, 4 * quad + 4)
+            nc.sync.dma_start(
+                out=side_planes[32 * quad : 32 * quad + 4, :].bitcast(I32),
+                in_=Wd_scales[0, rows4, :].bitcast(I32),
+            )
+            nc.sync.dma_start(
+                out=side_planes[32 * quad + 4 : 32 * quad + 12, 0:MOTORS].bitcast(I32),
+                in_=Wm_scales[:, rows4, :].bitcast(I32),
+            )
+
+        x_rows = load_rows(x, S_IN, "x_rows")
+        wd_words = keep.tile([P, 1, HID], U32, name="wd_words", align_bytes=64)
+        nc.sync.dma_start(out=wd_words[:].bitcast(I32), in_=packed_words(Wd_words))
+        c3_rows = load_rows(c3, HID, "c3_rows")
+
+        gate_words = {}
+        for half in range(HALVES):
+            for gate in GATE_ORDER:
+                col0 = gate * HID + half * N_TILE
+                for w, words in enumerate((Wih3_words, Whh3_words)):
+                    chunk = keep.tile(
+                        [P, 2, N_TILE], U32, name="gate_words_%d_%d_%d" % (w, half, gate), align_bytes=64
+                    )
+                    nc.sync.dma_start(
+                        out=chunk[:].bitcast(I32), in_=packed_words(words)[:, :, col0 : col0 + N_TILE]
+                    )
+                    gate_words[(w, half, gate)] = chunk
+        wm_words = keep.tile([P, 2, MOTORS], U32, name="wm_words", align_bytes=64)
+        nc.sync.dma_start(out=wm_words[:].bitcast(I32), in_=packed_words(Wm_words))
+
+        def quantise_rows(rows, g, name):
+            flipped = plain_pool.tile([P, BT, 2, P], F32, name="flipped_" + name, tag="plain")
+            for bt in range(BT):
+                pairs = rows[:, bt, :].bitcast(F32)
+                for u in range(2):
+                    nc.tensor.transpose(
+                        flipped[:, bt, u, :], pairs[:, 256 * g + u : 256 * (g + 1) : 2], ident_f32[:]
+                    )
+            grouped = keep.tile([P, BATCH * PACK], BF16, name="grouped_" + name, align_bytes=64)
+            nc.scalar.copy(
+                out=grouped[:].bitcast(F32).rearrange("p (bt b u) -> p bt b u", bt=BT, u=2),
+                in_=flipped[:].rearrange("p bt u b -> p bt b u"),
+            )
+            codes = keep.tile([P, BATCH], U32, name="codes_" + name, align_bytes=64)
+            plane = keep.tile([P, BATCH], U8, name="plane_" + name, align_bytes=64)
+            nc.vector.quantize_mx(out=codes[:].bitcast(FP8X4), scales=plane[:], in_=grouped[:])
+            return codes, plane
+
+        def mx_pass(acc, act, bt, words, plane, start, stop):
+            codes, act_plane = act
+            tile_cols = slice(bt * P, (bt + 1) * P)
+            nc.tensor.matmul_mx(
+                out=acc,
+                lhsT=codes[:, tile_cols].bitcast(FP8X4),
+                lhsT_scale=act_plane[:, tile_cols],
+                rhs=words.bitcast(FP8X4),
+                rhs_scale=plane,
+                start=start,
+                stop=stop,
+            )
+
+        gate_acts = {}
+        for w, rows in enumerate((y2_rows, h3_rows)):
+            for g in range(2):
+                gate_acts[(w, g)] = quantise_rows(rows, g, "gate_%d_%d" % (w, g))
+
+        def spread_bias(col0, piece, name):
+            bank = plain_pool.tile([P, N_TILE], F32, name="bank_" + name, tag="plain")
+            nc.tensor.matmul(bank[:], lhsT=ones[:], rhs=bias_rows[:, col0 : col0 + N_TILE], start=True, stop=True)
+            spread = keep.tile([P, N_TILE], F32, name=name)
+            if piece % 2 == 0:
+                nc.vector.tensor_copy(out=spread[:], in_=bank[:])
+            else:
+                nc.scalar.copy(out=spread[:], in_=bank[:])
+            return spread
+
+        gate_bias = {}
+        for half in range(HALVES):
+            for gate in GATE_ORDER:
+                gate_bias[(half, gate)] = spread_bias(
+                    gate * HID + half * N_TILE, len(gate_bias), "gate_bias_%d_%d" % (half, gate)
+                )
+        bd_spread = [spread_bias(GATE_COLS + half * N_TILE, half, "bd_spread_%d" % half) for half in range(HALVES)]
+        bm_spread = spread_bias(GATE_COLS + HID, 0, "bm_spread")
+
+        x_act = quantise_rows(x_rows, 0, "x")
+        skip = {}
+        for half in range(HALVES):
+            cols = slice(half * N_TILE, (half + 1) * N_TILE)
+            for bt in range(BT):
+                skip_acc = acc_pool.tile([P, N_TILE], F32, name="skip_acc", tag="acc")
+                mx_pass(skip_acc[:], x_act, bt, wd_words[:, 0, cols], side_planes[:, cols], True, True)
+                skip[(bt, half)] = keep.tile([P, N_TILE], F32, name="skip_%d_%d" % (bt, half))
+                nc.vector.tensor_tensor(
+                    out=skip[(bt, half)][:], in0=skip_acc[:], in1=bd_spread[half][:], op=ALU.add
+                )
+
+        value = {}
+        tanh_c = {}
+        mid = {}
+        half_passes = [(w, g) for w in range(2) for g in range(2)]
+
+        def gate_chunk(half, gate):
+            cols = slice(half * N_TILE, (half + 1) * N_TILE)
+            gate_cols = slice(gate * HID + half * N_TILE, gate * HID + (half + 1) * N_TILE)
+            accs = [acc_pool.tile([P, N_TILE], F32, name="gate_acc_%d" % bt, tag="acc") for bt in range(BT)]
+            for w, g in half_passes:
+                first = 8 * w + 4 * g
+                for bt in range(BT):
+                    mx_pass(
+                        accs[bt][:], gate_acts[(w, g)], bt,
+                        gate_words[(w, half, gate)][:, g, :], gate_planes[first:P, gate_cols],
+                        (w, g) == half_passes[0], (w, g) == half_passes[-1],
+                    )
+            for bt in range(BT):
+                out = keep.tile([P, N_TILE], F32, name="value_%d_%d" % (gate, bt))
+                nc.vector.tensor_tensor(out=out[:], in0=accs[bt][:], in1=gate_bias[(half, gate)][:], op=ALU.add)
+                nc.scalar.activation(out=out[:], in_=out[:], func=ACT.Tanh if gate == GATE_G else ACT.Sigmoid)
+                value[(gate, bt)] = out
+
+            if gate == GATE_F:
+                for bt in range(BT):
+                    kept = value[(GATE_F, bt)]
+                    nc.vector.tensor_tensor(out=kept[:], in0=kept[:], in1=c3_rows[:, bt, cols], op=ALU.mult)
+            if gate == GATE_G:
+                for bt in range(BT):
+                    fresh = value[(GATE_G, bt)]
+                    nc.vector.tensor_tensor(out=fresh[:], in0=fresh[:], in1=value[(GATE_I, bt)][:], op=ALU.mult)
+                for bt in range(BT):
+                    new_c = keep.tile([P, N_TILE], F32, name="new_c_%d_%d" % (bt, half))
+                    nc.vector.tensor_tensor(
+                        out=new_c[:], in0=value[(GATE_F, bt)][:], in1=value[(GATE_G, bt)][:], op=ALU.add
+                    )
+                    tanh_c[bt] = keep.tile([P, N_TILE], F32, name="tanh_c_%d" % bt)
+                    nc.scalar.activation(out=tanh_c[bt][:], in_=new_c[:], func=ACT.Tanh)
+                    nc.sync.dma_start(out=out_2[bt * P : (bt + 1) * P, cols], in_=new_c[:])
+            if gate == GATE_O:
+                y3 = {}
+                for bt in range(BT):
+                    y3[bt] = keep.tile([P, N_TILE], F32, name="y3_%d_%d" % (bt, half))
+                    nc.vector.tensor_tensor(out=y3[bt][:], in0=value[(GATE_O, bt)][:], in1=tanh_c[bt][:], op=ALU.mult)
+                for bt in range(BT):
+                    mid[(bt, half)] = keep.tile([P, N_TILE], BF16, name="mid_%d_%d" % (bt, half))
+                    nc.vector.tensor_tensor(out=mid[(bt, half)][:], in0=y3[bt][:], in1=skip[(bt, half)][:], op=ALU.add)
+                    nc.sync.dma_start(out=out_1[bt * P : (bt + 1) * P, cols], in_=y3[bt][:])
+
+        mid_act = {}
+
+        def flip_mid(half):
+            for bt in range(BT):
+                flipped = plain_pool.tile([P, PACK, P], BF16, name="flipped_mid", tag="plain")
+                for t in range(PACK):
+                    nc.tensor.transpose(flipped[:, t, :], mid[(bt, half)][:, t:N_TILE:PACK], ident_bf16[:])
+                grouped = keep.tile([P, P * PACK], BF16, name="grouped_mid_%d_%d" % (bt, half), align_bytes=64)
+                nc.scalar.copy(
+                    out=grouped[:].rearrange("p (b t) -> p b t", t=PACK), in_=flipped[:].rearrange("p t b -> p b t")
+                )
+                codes = keep.tile([P, P], U32, name="codes_mid_%d_%d" % (bt, half), align_bytes=64)
+                plane = keep.tile([P, P], U8, name="plane_mid_%d_%d" % (bt, half), align_bytes=64)
+                nc.vector.quantize_mx(out=codes[:].bitcast(FP8X4), scales=plane[:], in_=grouped[:])
+                mid_act[(bt, half)] = (codes, plane)
+
+        for half in range(HALVES):
+            for gate in GATE_ORDER:
+                gate_chunk(half, gate)
+                if half == 1 and gate == GATE_I:
+                    flip_mid(0)
+
+        nc.scalar.activation(out=table_warm[:], in_=zero_col[:], func=ACT.Exp)
+
+        motor_acc = [acc_pool.tile([P, MOTORS], F32, name="motor_acc_%d" % bt, tag="acc") for bt in range(BT)]
+
+        def motor_passes(g):
+            for bt in range(BT):
+                mx_pass(
+                    motor_acc[bt][:], mid_act[(bt, g)], 0,
+                    wm_words[:, g, :], side_planes[4 + 4 * g : P, 0:MOTORS], g == 0, g == 1,
+                )
+
+        motor_passes(0)
+        flip_mid(1)
+        motor_passes(1)
+
+        row_max = keep.tile([P, BT], F32, name="row_max")
+        neg_max = keep.tile([P, BT], F32, name="neg_max")
+        sum_exp = keep.tile([P, BT], F32, name="sum_exp")
+        log_sum = keep.tile([P, BT], F32, name="log_sum")
+        motors = [keep.tile([P, MOTORS], F32, name="motors_%d" % bt) for bt in range(BT)]
+        for bt in range(BT):
+            nc.vector.tensor_tensor(out=motors[bt][:], in0=motor_acc[bt][:], in1=bm_spread[:], op=ALU.add)
+        for bt in range(BT):
+            nc.vector.tensor_reduce(out=row_max[:, bt : bt + 1], in_=motors[bt][:], axis=AXIS.X, op=ALU.max)
+        nc.vector.tensor_scalar_mul(out=neg_max[:], in0=row_max[:], scalar1=-1.0)
+        for bt in range(BT):
+            exps = keep.tile([P, MOTORS], F32, name="exps_%d" % bt)
+            nc.scalar.activation(
+                out=exps[:], in_=motors[bt][:], func=ACT.Exp,
+                bias=neg_max[:, bt : bt + 1], scale=1.0, accum_out=sum_exp[:, bt : bt + 1],
+            )
+        nc.scalar.activation(out=log_sum[:], in_=sum_exp[:], func=ACT.Ln)
+        for bt in range(BT):
+            preds = keep.tile([P, MOTORS], F32, name="preds_%d" % bt)
+            nc.vector.tensor_scalar(
+                out=preds[:], in0=motors[bt][:],
+                scalar1=row_max[:, bt : bt + 1], scalar2=log_sum[:, bt : bt + 1],
+                op0=ALU.subtract, op1=ALU.subtract,
+            )
+            nc.sync.dma_start(out=out_0[bt * P : (bt + 1) * P, :], in_=preds[:])

@@ -28,7 +28,12 @@ HALVES = HID // N_TILE
 GATE_I, GATE_F, GATE_G, GATE_O = 0, 1, 2, 3
 GATE_ORDER = (GATE_F, GATE_I, GATE_G, GATE_O)
 GATE_COLS = 4 * HID
-BIAS_COLS = GATE_COLS + HID + MOTORS
+GATE_PIECES = GATE_COLS // N_TILE
+BIAS_ROW_IH = 0
+BIAS_ROW_HH = BIAS_ROW_IH + GATE_PIECES
+BIAS_ROW_D = BIAS_ROW_HH + GATE_PIECES
+BIAS_ROW_M = BIAS_ROW_D + HALVES
+SCALES_PER_LOAD = 4
 
 FLOPS = 2 * BATCH * (2 * HID * GATE_COLS + S_IN * HID + HID * MOTORS)
 
@@ -46,36 +51,53 @@ def tile_network_pb_kernel(
     nc = tc.nc
     with ExitStack() as stack:
         keep = stack.enter_context(tc.tile_pool(name="keep", bufs=1))
-        acc_pool = stack.enter_context(tc.psum_pool(name="acc", bufs=6))
-        plain_pool = stack.enter_context(tc.psum_pool(name="plain", bufs=2))
+        acc_pool = stack.enter_context(tc.psum_pool(name="acc", bufs=4))
+        plain_pool = stack.enter_context(tc.psum_pool(name="plain", bufs=4))
         stack.enter_context(tc.manual_schedule())
 
+        zero_col = keep.tile([P, 1], F32, name="zero_col")
+        nc.vector.memset(zero_col[:], 0.0)
         gate_planes = keep.tile([P, GATE_COLS], U8, name="gate_planes", align_bytes=64)
         side_planes = keep.tile([P, HID], U8, name="side_planes", align_bytes=64)
         nc.vector.memset(gate_planes[:].bitcast(I32), 0)
         nc.vector.memset(side_planes[:].bitcast(I32), 0)
-        bias_rows = keep.tile([P, BIAS_COLS], BF16, name="bias_rows")
+        bias_rows = keep.tile([P, N_TILE], BF16, name="bias_rows")
         nc.vector.memset(bias_rows[:].bitcast(I32), 0)
-        zero_col = keep.tile([P, 1], F32, name="zero_col")
-        nc.vector.memset(zero_col[:], 0.0)
 
         ident_f32 = keep.tile([P, P], F32, name="ident_f32")
         make_identity(nc, ident_f32[:])
         ident_bf16 = keep.tile([P, P], BF16, name="ident_bf16")
         make_identity(nc, ident_bf16[:])
-        ones = keep.tile([P, P], BF16, name="ones")
-        nc.gpsimd.memset(ones[:], 1.0)
+        gate_pick = keep.tile([P, GATE_PIECES], BF16, name="gate_pick")
+        nc.gpsimd.tensor_tensor(
+            out=gate_pick[:],
+            in0=ident_bf16[:, BIAS_ROW_IH : BIAS_ROW_IH + GATE_PIECES],
+            in1=ident_bf16[:, BIAS_ROW_HH : BIAS_ROW_HH + GATE_PIECES],
+            op=ALU.add,
+        )
 
-        nc.scalar.dma_start(out=bias_rows[0:1, 0:GATE_COLS], in_=bih3.rearrange("(o n) -> o n", o=1))
-        nc.scalar.dma_start(out=bias_rows[1:2, 0:GATE_COLS], in_=bhh3.rearrange("(o n) -> o n", o=1))
-        nc.scalar.dma_start(
-            out=bias_rows[0:1, GATE_COLS : GATE_COLS + HID], in_=bd.rearrange("(o n) -> o n", o=1)
-        )
-        nc.scalar.dma_start(
-            out=bias_rows[0:1, GATE_COLS + HID : BIAS_COLS], in_=bm.rearrange("(o n) -> o n", o=1)
-        )
         table_warm = keep.tile([P, 1], F32, name="table_warm")
         nc.scalar.activation(out=table_warm[:], in_=zero_col[:], func=ACT.Sigmoid)
+        for row0, vector in ((BIAS_ROW_IH, bih3), (BIAS_ROW_HH, bhh3), (BIAS_ROW_D, bd), (BIAS_ROW_M, bm)):
+            pieces = vector.rearrange("(r n) -> r n", n=N_TILE)
+            nc.scalar.dma_start(out=bias_rows[row0 : row0 + pieces.shape[0], :], in_=pieces)
+
+        scale_loads = []
+        for quad in range(QUADS):
+            rows4 = slice(4 * quad, 4 * quad + 4)
+            for w, scales in enumerate((Wih3_scales, Whh3_scales)):
+                first = 32 * quad + 8 * w
+                scale_loads.append((gate_planes[first : first + 8, :], scales[:, rows4, :]))
+        for quad in range(QUADS):
+            rows4 = slice(4 * quad, 4 * quad + 4)
+            scale_loads.append((side_planes[32 * quad : 32 * quad + 4, :], Wd_scales[0, rows4, :]))
+        for quad in range(QUADS):
+            rows4 = slice(4 * quad, 4 * quad + 4)
+            scale_loads.append((side_planes[32 * quad + 4 : 32 * quad + 12, 0:MOTORS], Wm_scales[:, rows4, :]))
+
+        def load_scales(group):
+            for sbuf_rows, dram_rows in scale_loads[group * SCALES_PER_LOAD : (group + 1) * SCALES_PER_LOAD]:
+                nc.sync.dma_start(out=sbuf_rows.bitcast(I32), in_=dram_rows.bitcast(I32))
 
         def load_rows(src, width, name):
             rows = keep.tile([P, BT, width], BF16, name=name)
@@ -83,30 +105,14 @@ def tile_network_pb_kernel(
             return rows
 
         y2_rows = load_rows(y2, HID, "y2_rows")
+        load_scales(0)
         h3_rows = load_rows(h3, HID, "h3_rows")
-
-        for quad in range(QUADS):
-            rows4 = slice(4 * quad, 4 * quad + 4)
-            for w, scales in enumerate((Wih3_scales, Whh3_scales)):
-                first = 32 * quad + 8 * w
-                nc.sync.dma_start(
-                    out=gate_planes[first : first + 8, :].bitcast(I32),
-                    in_=scales[:, rows4, :].bitcast(I32),
-                )
-        for quad in range(QUADS):
-            rows4 = slice(4 * quad, 4 * quad + 4)
-            nc.sync.dma_start(
-                out=side_planes[32 * quad : 32 * quad + 4, :].bitcast(I32),
-                in_=Wd_scales[0, rows4, :].bitcast(I32),
-            )
-            nc.sync.dma_start(
-                out=side_planes[32 * quad + 4 : 32 * quad + 12, 0:MOTORS].bitcast(I32),
-                in_=Wm_scales[:, rows4, :].bitcast(I32),
-            )
-
+        load_scales(1)
         x_rows = load_rows(x, S_IN, "x_rows")
+        load_scales(2)
         wd_words = keep.tile([P, 1, HID], U32, name="wd_words", align_bytes=64)
         nc.sync.dma_start(out=wd_words[:].bitcast(I32), in_=packed_words(Wd_words))
+        load_scales(3)
         c3_rows = load_rows(c3, HID, "c3_rows")
 
         gate_words = {}
@@ -124,6 +130,12 @@ def tile_network_pb_kernel(
         wm_words = keep.tile([P, 2, MOTORS], U32, name="wm_words", align_bytes=64)
         nc.sync.dma_start(out=wm_words[:].bitcast(I32), in_=packed_words(Wm_words))
 
+        def copy_out(on_vector, out, in_):
+            if on_vector:
+                nc.vector.tensor_copy(out=out, in_=in_)
+            else:
+                nc.scalar.copy(out=out, in_=in_)
+
         def quantise_rows(rows, g, name):
             flipped = plain_pool.tile([P, BT, 2, P], F32, name="flipped_" + name, tag="plain")
             for bt in range(BT):
@@ -133,9 +145,10 @@ def tile_network_pb_kernel(
                         flipped[:, bt, u, :], pairs[:, 256 * g + u : 256 * (g + 1) : 2], ident_f32[:]
                     )
             grouped = keep.tile([P, BATCH * PACK], BF16, name="grouped_" + name, align_bytes=64)
-            nc.scalar.copy(
-                out=grouped[:].bitcast(F32).rearrange("p (bt b u) -> p bt b u", bt=BT, u=2),
-                in_=flipped[:].rearrange("p bt u b -> p bt b u"),
+            copy_out(
+                g % 2 == 1,
+                grouped[:].bitcast(F32).rearrange("p (bt b u) -> p bt b u", bt=BT, u=2),
+                flipped[:].rearrange("p bt u b -> p bt b u"),
             )
             codes = keep.tile([P, BATCH], U32, name="codes_" + name, align_bytes=64)
             plane = keep.tile([P, BATCH], U8, name="plane_" + name, align_bytes=64)
@@ -160,24 +173,24 @@ def tile_network_pb_kernel(
             for g in range(2):
                 gate_acts[(w, g)] = quantise_rows(rows, g, "gate_%d_%d" % (w, g))
 
-        def spread_bias(col0, piece, name):
+        def spread_bias(pick, on_vector, name):
             bank = plain_pool.tile([P, N_TILE], F32, name="bank_" + name, tag="plain")
-            nc.tensor.matmul(bank[:], lhsT=ones[:], rhs=bias_rows[:, col0 : col0 + N_TILE], start=True, stop=True)
+            nc.tensor.matmul(bank[:], lhsT=pick.to_broadcast([P, P]), rhs=bias_rows[:], start=True, stop=True)
             spread = keep.tile([P, N_TILE], F32, name=name)
-            if piece % 2 == 0:
-                nc.vector.tensor_copy(out=spread[:], in_=bank[:])
-            else:
-                nc.scalar.copy(out=spread[:], in_=bank[:])
+            copy_out(on_vector, spread[:], bank[:])
             return spread
 
+        def spread_gate_bias(half, gate, on_vector):
+            piece = 2 * gate + half
+            return spread_bias(gate_pick[:, piece : piece + 1], on_vector, "gate_bias_%d_%d" % (half, gate))
+
         gate_bias = {}
-        for half in range(HALVES):
-            for gate in GATE_ORDER:
-                gate_bias[(half, gate)] = spread_bias(
-                    gate * HID + half * N_TILE, len(gate_bias), "gate_bias_%d_%d" % (half, gate)
-                )
-        bd_spread = [spread_bias(GATE_COLS + half * N_TILE, half, "bd_spread_%d" % half) for half in range(HALVES)]
-        bm_spread = spread_bias(GATE_COLS + HID, 0, "bm_spread")
+        for gate in GATE_ORDER:
+            gate_bias[(0, gate)] = spread_gate_bias(0, gate, gate % 2 == 1)
+        bd_spread = [
+            spread_bias(ident_bf16[:, BIAS_ROW_D + half : BIAS_ROW_D + half + 1], half % 2 == 1, "bd_spread_%d" % half)
+            for half in range(HALVES)
+        ]
 
         x_act = quantise_rows(x_rows, 0, "x")
         skip = {}
@@ -217,7 +230,7 @@ def tile_network_pb_kernel(
             if gate == GATE_F:
                 for bt in range(BT):
                     kept = value[(GATE_F, bt)]
-                    nc.vector.tensor_tensor(out=kept[:], in0=kept[:], in1=c3_rows[:, bt, cols], op=ALU.mult)
+                    nc.gpsimd.tensor_tensor(out=kept[:], in0=kept[:], in1=c3_rows[:, bt, cols], op=ALU.mult)
             if gate == GATE_G:
                 for bt in range(BT):
                     fresh = value[(GATE_G, bt)]
@@ -259,8 +272,11 @@ def tile_network_pb_kernel(
         for half in range(HALVES):
             for gate in GATE_ORDER:
                 gate_chunk(half, gate)
+                if half == 0:
+                    gate_bias[(1, gate)] = spread_gate_bias(1, gate, False)
                 if half == 1 and gate == GATE_I:
                     flip_mid(0)
+                    bm_spread = spread_bias(ident_bf16[:, BIAS_ROW_M : BIAS_ROW_M + 1], False, "bm_spread")
 
         nc.scalar.activation(out=table_warm[:], in_=zero_col[:], func=ACT.Exp)
 

@@ -27,13 +27,14 @@ MOTORS = 512
 HALVES = HID // N_TILE
 GATE_I, GATE_F, GATE_G, GATE_O = 0, 1, 2, 3
 GATE_ORDER = (GATE_F, GATE_I, GATE_G, GATE_O)
+GATE_CHUNKS = [(half, gate) for half in range(HALVES) for gate in GATE_ORDER]
 GATE_COLS = 4 * HID
 GATE_PIECES = GATE_COLS // N_TILE
 BIAS_ROW_IH = 0
 BIAS_ROW_HH = BIAS_ROW_IH + GATE_PIECES
 BIAS_ROW_D = BIAS_ROW_HH + GATE_PIECES
 BIAS_ROW_M = BIAS_ROW_D + HALVES
-SCALES_PER_LOAD = 4
+FIRST_IH, FIRST_HH = 0, 8
 
 FLOPS = 2 * BATCH * (2 * HID * GATE_COLS + S_IN * HID + HID * MOTORS)
 
@@ -51,21 +52,20 @@ def tile_network_pb_kernel(
     nc = tc.nc
     with ExitStack() as stack:
         keep = stack.enter_context(tc.tile_pool(name="keep", bufs=1))
-        acc_pool = stack.enter_context(tc.psum_pool(name="acc", bufs=4))
-        plain_pool = stack.enter_context(tc.psum_pool(name="plain", bufs=4))
+        psum = stack.enter_context(tc.psum_pool(name="psum", bufs=8))
         stack.enter_context(tc.manual_schedule())
 
+        bias_rows = keep.tile([P, N_TILE], BF16, name="bias_rows")
+        nc.vector.memset(bias_rows[:].bitcast(I32), 0)
         zero_col = keep.tile([P, 1], F32, name="zero_col")
         nc.vector.memset(zero_col[:], 0.0)
         gate_planes = keep.tile([P, GATE_COLS], U8, name="gate_planes", align_bytes=64)
-        side_planes = keep.tile([P, HID], U8, name="side_planes", align_bytes=64)
+        wd_planes = keep.tile([P, HID], U8, name="wd_planes", align_bytes=64)
+        wm_planes = keep.tile([P, MOTORS], U8, name="wm_planes", align_bytes=64)
         nc.vector.memset(gate_planes[:].bitcast(I32), 0)
-        nc.vector.memset(side_planes[:].bitcast(I32), 0)
-        bias_rows = keep.tile([P, N_TILE], BF16, name="bias_rows")
-        nc.vector.memset(bias_rows[:].bitcast(I32), 0)
+        nc.vector.memset(wd_planes[:].bitcast(I32), 0)
+        nc.vector.memset(wm_planes[:].bitcast(I32), 0)
 
-        ident_f32 = keep.tile([P, P], F32, name="ident_f32")
-        make_identity(nc, ident_f32[:])
         ident_bf16 = keep.tile([P, P], BF16, name="ident_bf16")
         make_identity(nc, ident_bf16[:])
         gate_pick = keep.tile([P, GATE_PIECES], BF16, name="gate_pick")
@@ -75,58 +75,54 @@ def tile_network_pb_kernel(
             in1=ident_bf16[:, BIAS_ROW_HH : BIAS_ROW_HH + GATE_PIECES],
             op=ALU.add,
         )
+        ident_f32 = keep.tile([P, P], F32, name="ident_f32")
+        make_identity(nc, ident_f32[:])
 
         table_warm = keep.tile([P, 1], F32, name="table_warm")
         nc.scalar.activation(out=table_warm[:], in_=zero_col[:], func=ACT.Sigmoid)
-        for row0, vector in ((BIAS_ROW_IH, bih3), (BIAS_ROW_HH, bhh3), (BIAS_ROW_D, bd), (BIAS_ROW_M, bm)):
-            pieces = vector.rearrange("(r n) -> r n", n=N_TILE)
-            nc.scalar.dma_start(out=bias_rows[row0 : row0 + pieces.shape[0], :], in_=pieces)
-
-        scale_loads = []
-        for quad in range(QUADS):
-            rows4 = slice(4 * quad, 4 * quad + 4)
-            for w, scales in enumerate((Wih3_scales, Whh3_scales)):
-                first = 32 * quad + 8 * w
-                scale_loads.append((gate_planes[first : first + 8, :], scales[:, rows4, :]))
-        for quad in range(QUADS):
-            rows4 = slice(4 * quad, 4 * quad + 4)
-            scale_loads.append((side_planes[32 * quad : 32 * quad + 4, :], Wd_scales[0, rows4, :]))
-        for quad in range(QUADS):
-            rows4 = slice(4 * quad, 4 * quad + 4)
-            scale_loads.append((side_planes[32 * quad + 4 : 32 * quad + 12, 0:MOTORS], Wm_scales[:, rows4, :]))
-
-        def load_scales(group):
-            for sbuf_rows, dram_rows in scale_loads[group * SCALES_PER_LOAD : (group + 1) * SCALES_PER_LOAD]:
-                nc.sync.dma_start(out=sbuf_rows.bitcast(I32), in_=dram_rows.bitcast(I32))
 
         def load_rows(src, width, name):
             rows = keep.tile([P, BT, width], BF16, name=name)
             nc.sync.dma_start(out=rows[:], in_=src.rearrange("(bt p) k -> p bt k", p=P))
             return rows
 
-        y2_rows = load_rows(y2, HID, "y2_rows")
-        load_scales(0)
-        h3_rows = load_rows(h3, HID, "h3_rows")
-        load_scales(1)
-        x_rows = load_rows(x, S_IN, "x_rows")
-        load_scales(2)
-        wd_words = keep.tile([P, 1, HID], U32, name="wd_words", align_bytes=64)
-        nc.sync.dma_start(out=wd_words[:].bitcast(I32), in_=packed_words(Wd_words))
-        load_scales(3)
-        c3_rows = load_rows(c3, HID, "c3_rows")
+        def load_scales(plane_tile, first, scales):
+            passes = scales.shape[0]
+            for quad in range(QUADS):
+                top = 32 * quad + first
+                nc.sync.dma_start(
+                    out=plane_tile[top : top + 4 * passes, :].bitcast(I32),
+                    in_=scales[:, 4 * quad : 4 * quad + 4, :].bitcast(I32),
+                )
+
+        def load_bias(row0, vector):
+            pieces = vector.rearrange("(r n) -> r n", n=N_TILE)
+            nc.sync.dma_start(out=bias_rows[row0 : row0 + pieces.shape[0], :], in_=pieces)
 
         gate_words = {}
-        for half in range(HALVES):
-            for gate in GATE_ORDER:
-                col0 = gate * HID + half * N_TILE
-                for w, words in enumerate((Wih3_words, Whh3_words)):
-                    chunk = keep.tile(
-                        [P, 2, N_TILE], U32, name="gate_words_%d_%d_%d" % (w, half, gate), align_bytes=64
-                    )
-                    nc.sync.dma_start(
-                        out=chunk[:].bitcast(I32), in_=packed_words(words)[:, :, col0 : col0 + N_TILE]
-                    )
-                    gate_words[(w, half, gate)] = chunk
+
+        def load_gate_chunk(half, gate):
+            col0 = gate * HID + half * N_TILE
+            for w, words in enumerate((Wih3_words, Whh3_words)):
+                chunk = keep.tile([P, 2, N_TILE], U32, name="gate_words_%d_%d_%d" % (w, half, gate), align_bytes=64)
+                nc.sync.dma_start(out=chunk[:].bitcast(I32), in_=packed_words(words)[:, :, col0 : col0 + N_TILE])
+                gate_words[(w, half, gate)] = chunk
+
+        for row0, vector in ((BIAS_ROW_IH, bih3), (BIAS_ROW_HH, bhh3), (BIAS_ROW_D, bd), (BIAS_ROW_M, bm)):
+            load_bias(row0, vector)
+        y2_rows = load_rows(y2, HID, "y2_rows")
+        h3_rows = load_rows(h3, HID, "h3_rows")
+        load_scales(gate_planes, FIRST_IH, Wih3_scales)
+        load_scales(gate_planes, FIRST_HH, Whh3_scales)
+        x_rows = load_rows(x, S_IN, "x_rows")
+        wd_words = keep.tile([P, 1, HID], U32, name="wd_words", align_bytes=64)
+        nc.sync.dma_start(out=wd_words[:].bitcast(I32), in_=packed_words(Wd_words))
+        load_scales(wd_planes, 0, Wd_scales)
+        c3_rows = load_rows(c3, HID, "c3_rows")
+        for half, gate in GATE_CHUNKS:
+            load_gate_chunk(half, gate)
+            if (half, gate) == (1, GATE_I):
+                load_scales(wm_planes, 0, Wm_scales)
         wm_words = keep.tile([P, 2, MOTORS], U32, name="wm_words", align_bytes=64)
         nc.sync.dma_start(out=wm_words[:].bitcast(I32), in_=packed_words(Wm_words))
 
@@ -136,8 +132,8 @@ def tile_network_pb_kernel(
             else:
                 nc.scalar.copy(out=out, in_=in_)
 
-        def quantise_rows(rows, g, name):
-            flipped = plain_pool.tile([P, BT, 2, P], F32, name="flipped_" + name, tag="plain")
+        def quantise_rows(rows, g, on_vector, name):
+            flipped = psum.tile([P, BT, 2, P], F32, name="flipped_" + name, tag="bank")
             for bt in range(BT):
                 pairs = rows[:, bt, :].bitcast(F32)
                 for u in range(2):
@@ -146,7 +142,7 @@ def tile_network_pb_kernel(
                     )
             grouped = keep.tile([P, BATCH * PACK], BF16, name="grouped_" + name, align_bytes=64)
             copy_out(
-                g % 2 == 1,
+                on_vector,
                 grouped[:].bitcast(F32).rearrange("p (bt b u) -> p bt b u", bt=BT, u=2),
                 flipped[:].rearrange("p bt u b -> p bt b u"),
             )
@@ -168,41 +164,42 @@ def tile_network_pb_kernel(
                 stop=stop,
             )
 
-        gate_acts = {}
-        for w, rows in enumerate((y2_rows, h3_rows)):
-            for g in range(2):
-                gate_acts[(w, g)] = quantise_rows(rows, g, "gate_%d_%d" % (w, g))
-
         def spread_bias(pick, on_vector, name):
-            bank = plain_pool.tile([P, N_TILE], F32, name="bank_" + name, tag="plain")
+            bank = psum.tile([P, N_TILE], F32, name="bank_" + name, tag="bank")
             nc.tensor.matmul(bank[:], lhsT=pick.to_broadcast([P, P]), rhs=bias_rows[:], start=True, stop=True)
             spread = keep.tile([P, N_TILE], F32, name=name)
             copy_out(on_vector, spread[:], bank[:])
             return spread
 
-        def spread_gate_bias(half, gate, on_vector):
-            piece = 2 * gate + half
-            return spread_bias(gate_pick[:, piece : piece + 1], on_vector, "gate_bias_%d_%d" % (half, gate))
-
         gate_bias = {}
-        for gate in GATE_ORDER:
-            gate_bias[(0, gate)] = spread_gate_bias(0, gate, gate % 2 == 1)
+
+        def spread_gate_biases(half, on_vector):
+            for gate in GATE_ORDER:
+                piece = 2 * gate + half
+                gate_bias[(half, gate)] = spread_bias(
+                    gate_pick[:, piece : piece + 1], on_vector, "gate_bias_%d_%d" % (half, gate)
+                )
+
+        spread_gate_biases(0, True)
+        gate_acts = {}
+        for w, rows in enumerate((y2_rows, h3_rows)):
+            for g in range(2):
+                gate_acts[(w, g)] = quantise_rows(rows, g, False, "gate_%d_%d" % (w, g))
         bd_spread = [
-            spread_bias(ident_bf16[:, BIAS_ROW_D + half : BIAS_ROW_D + half + 1], half % 2 == 1, "bd_spread_%d" % half)
+            spread_bias(ident_bf16[:, BIAS_ROW_D + half : BIAS_ROW_D + half + 1], False, "bd_spread_%d" % half)
             for half in range(HALVES)
         ]
+        x_act = quantise_rows(x_rows, 0, True, "x")
+        spread_gate_biases(1, False)
 
-        x_act = quantise_rows(x_rows, 0, "x")
         skip = {}
         for half in range(HALVES):
             cols = slice(half * N_TILE, (half + 1) * N_TILE)
             for bt in range(BT):
-                skip_acc = acc_pool.tile([P, N_TILE], F32, name="skip_acc", tag="acc")
-                mx_pass(skip_acc[:], x_act, bt, wd_words[:, 0, cols], side_planes[:, cols], True, True)
+                skip_acc = psum.tile([P, N_TILE], F32, name="skip_acc", tag="bank")
+                mx_pass(skip_acc[:], x_act, bt, wd_words[:, 0, cols], wd_planes[:, cols], True, True)
                 skip[(bt, half)] = keep.tile([P, N_TILE], F32, name="skip_%d_%d" % (bt, half))
-                nc.vector.tensor_tensor(
-                    out=skip[(bt, half)][:], in0=skip_acc[:], in1=bd_spread[half][:], op=ALU.add
-                )
+                nc.vector.tensor_tensor(out=skip[(bt, half)][:], in0=skip_acc[:], in1=bd_spread[half][:], op=ALU.add)
 
         value = {}
         tanh_c = {}
@@ -212,9 +209,9 @@ def tile_network_pb_kernel(
         def gate_chunk(half, gate):
             cols = slice(half * N_TILE, (half + 1) * N_TILE)
             gate_cols = slice(gate * HID + half * N_TILE, gate * HID + (half + 1) * N_TILE)
-            accs = [acc_pool.tile([P, N_TILE], F32, name="gate_acc_%d" % bt, tag="acc") for bt in range(BT)]
+            accs = [psum.tile([P, N_TILE], F32, name="gate_acc_%d" % bt, tag="bank") for bt in range(BT)]
             for w, g in half_passes:
-                first = 8 * w + 4 * g
+                first = (FIRST_IH, FIRST_HH)[w] + 4 * g
                 for bt in range(BT):
                     mx_pass(
                         accs[bt][:], gate_acts[(w, g)], bt,
@@ -243,21 +240,23 @@ def tile_network_pb_kernel(
                     tanh_c[bt] = keep.tile([P, N_TILE], F32, name="tanh_c_%d" % bt)
                     nc.scalar.activation(out=tanh_c[bt][:], in_=new_c[:], func=ACT.Tanh)
                     nc.sync.dma_start(out=out_2[bt * P : (bt + 1) * P, cols], in_=new_c[:])
-            if gate == GATE_O:
-                y3 = {}
-                for bt in range(BT):
-                    y3[bt] = keep.tile([P, N_TILE], F32, name="y3_%d_%d" % (bt, half))
-                    nc.vector.tensor_tensor(out=y3[bt][:], in0=value[(GATE_O, bt)][:], in1=tanh_c[bt][:], op=ALU.mult)
-                for bt in range(BT):
-                    mid[(bt, half)] = keep.tile([P, N_TILE], BF16, name="mid_%d_%d" % (bt, half))
-                    nc.vector.tensor_tensor(out=mid[(bt, half)][:], in0=y3[bt][:], in1=skip[(bt, half)][:], op=ALU.add)
-                    nc.sync.dma_start(out=out_1[bt * P : (bt + 1) * P, cols], in_=y3[bt][:])
+
+        def hidden_output(half, engine):
+            cols = slice(half * N_TILE, (half + 1) * N_TILE)
+            y3 = {}
+            for bt in range(BT):
+                y3[bt] = keep.tile([P, N_TILE], F32, name="y3_%d_%d" % (bt, half))
+                engine.tensor_tensor(out=y3[bt][:], in0=value[(GATE_O, bt)][:], in1=tanh_c[bt][:], op=ALU.mult)
+            for bt in range(BT):
+                mid[(bt, half)] = keep.tile([P, N_TILE], BF16, name="mid_%d_%d" % (bt, half))
+                engine.tensor_tensor(out=mid[(bt, half)][:], in0=y3[bt][:], in1=skip[(bt, half)][:], op=ALU.add)
+                nc.sync.dma_start(out=out_1[bt * P : (bt + 1) * P, cols], in_=y3[bt][:])
 
         mid_act = {}
 
         def flip_mid(half):
             for bt in range(BT):
-                flipped = plain_pool.tile([P, PACK, P], BF16, name="flipped_mid", tag="plain")
+                flipped = psum.tile([P, PACK, P], BF16, name="flipped_mid", tag="bank")
                 for t in range(PACK):
                     nc.tensor.transpose(flipped[:, t, :], mid[(bt, half)][:, t:N_TILE:PACK], ident_bf16[:])
                 grouped = keep.tile([P, P * PACK], BF16, name="grouped_mid_%d_%d" % (bt, half), align_bytes=64)
@@ -269,29 +268,23 @@ def tile_network_pb_kernel(
                 nc.vector.quantize_mx(out=codes[:].bitcast(FP8X4), scales=plane[:], in_=grouped[:])
                 mid_act[(bt, half)] = (codes, plane)
 
+        for half, gate in GATE_CHUNKS:
+            gate_chunk(half, gate)
+            if (half, gate) == (1, GATE_F):
+                hidden_output(0, nc.gpsimd)
+        hidden_output(1, nc.vector)
+        bm_spread = spread_bias(ident_bf16[:, BIAS_ROW_M : BIAS_ROW_M + 1], False, "bm_spread")
+
         for half in range(HALVES):
-            for gate in GATE_ORDER:
-                gate_chunk(half, gate)
-                if half == 0:
-                    gate_bias[(1, gate)] = spread_gate_bias(1, gate, False)
-                if half == 1 and gate == GATE_I:
-                    flip_mid(0)
-                    bm_spread = spread_bias(ident_bf16[:, BIAS_ROW_M : BIAS_ROW_M + 1], False, "bm_spread")
-
+            flip_mid(half)
         nc.scalar.activation(out=table_warm[:], in_=zero_col[:], func=ACT.Exp)
-
-        motor_acc = [acc_pool.tile([P, MOTORS], F32, name="motor_acc_%d" % bt, tag="acc") for bt in range(BT)]
-
-        def motor_passes(g):
+        motor_acc = [psum.tile([P, MOTORS], F32, name="motor_acc_%d" % bt, tag="bank") for bt in range(BT)]
+        for g in range(HALVES):
             for bt in range(BT):
                 mx_pass(
                     motor_acc[bt][:], mid_act[(bt, g)], 0,
-                    wm_words[:, g, :], side_planes[4 + 4 * g : P, 0:MOTORS], g == 0, g == 1,
+                    wm_words[:, g, :], wm_planes[4 * g : P, :], g == 0, g == HALVES - 1,
                 )
-
-        motor_passes(0)
-        flip_mid(1)
-        motor_passes(1)
 
         row_max = keep.tile([P, BT], F32, name="row_max")
         neg_max = keep.tile([P, BT], F32, name="neg_max")
@@ -302,7 +295,7 @@ def tile_network_pb_kernel(
             nc.vector.tensor_tensor(out=motors[bt][:], in0=motor_acc[bt][:], in1=bm_spread[:], op=ALU.add)
         for bt in range(BT):
             nc.vector.tensor_reduce(out=row_max[:, bt : bt + 1], in_=motors[bt][:], axis=AXIS.X, op=ALU.max)
-        nc.vector.tensor_scalar_mul(out=neg_max[:], in0=row_max[:], scalar1=-1.0)
+            nc.vector.tensor_scalar_mul(out=neg_max[:, bt : bt + 1], in0=row_max[:, bt : bt + 1], scalar1=-1.0)
         for bt in range(BT):
             exps = keep.tile([P, MOTORS], F32, name="exps_%d" % bt)
             nc.scalar.activation(

@@ -34,7 +34,6 @@ BIAS_ROW_IH = 0
 BIAS_ROW_HH = BIAS_ROW_IH + GATE_PIECES
 BIAS_ROW_D = BIAS_ROW_HH + GATE_PIECES
 BIAS_ROW_M = BIAS_ROW_D + HALVES
-FIRST_IH, FIRST_HH = 0, 8
 
 FLOPS = 2 * BATCH * (2 * HID * GATE_COLS + S_IN * HID + HID * MOTORS)
 
@@ -59,10 +58,13 @@ def tile_network_pb_kernel(
         nc.vector.memset(bias_rows[:].bitcast(I32), 0)
         zero_col = keep.tile([P, 1], F32, name="zero_col")
         nc.vector.memset(zero_col[:], 0.0)
-        gate_planes = keep.tile([P, GATE_COLS], U8, name="gate_planes", align_bytes=64)
+        gate_planes = {}
+        for w in range(2):
+            for g in range(2):
+                gate_planes[(w, g)] = keep.tile([P, HID], U8, name="gate_planes_%d_%d" % (w, g), align_bytes=64)
+                nc.vector.memset(gate_planes[(w, g)][:].bitcast(I32), 0)
         wd_planes = keep.tile([P, HID], U8, name="wd_planes", align_bytes=64)
         wm_planes = keep.tile([P, MOTORS], U8, name="wm_planes", align_bytes=64)
-        nc.vector.memset(gate_planes[:].bitcast(I32), 0)
         nc.vector.memset(wd_planes[:].bitcast(I32), 0)
         nc.vector.memset(wm_planes[:].bitcast(I32), 0)
 
@@ -95,6 +97,14 @@ def tile_network_pb_kernel(
                     in_=scales[:, 4 * quad : 4 * quad + 4, :].bitcast(I32),
                 )
 
+        def load_gate_scales(w, g):
+            scales = (Wih3_scales, Whh3_scales)[w]
+            for quad in range(QUADS):
+                nc.sync.dma_start(
+                    out=gate_planes[(w, g)][32 * quad : 32 * quad + 16, :].bitcast(I32),
+                    in_=scales[g, 4 * quad : 4 * quad + 4, :].rearrange("r (j c) -> j r c", j=4).bitcast(I32),
+                )
+
         def load_bias(row0, vector):
             pieces = vector.rearrange("(r n) -> r n", n=N_TILE)
             nc.sync.dma_start(out=bias_rows[row0 : row0 + pieces.shape[0], :], in_=pieces)
@@ -112,8 +122,9 @@ def tile_network_pb_kernel(
             load_bias(row0, vector)
         y2_rows = load_rows(y2, HID, "y2_rows")
         h3_rows = load_rows(h3, HID, "h3_rows")
-        load_scales(gate_planes, FIRST_IH, Wih3_scales)
-        load_scales(gate_planes, FIRST_HH, Whh3_scales)
+        for w in range(2):
+            for g in range(2):
+                load_gate_scales(w, g)
         x_rows = load_rows(x, S_IN, "x_rows")
         wd_words = keep.tile([P, 1, HID], U32, name="wd_words", align_bytes=64)
         nc.sync.dma_start(out=wd_words[:].bitcast(I32), in_=packed_words(Wd_words))
@@ -208,14 +219,12 @@ def tile_network_pb_kernel(
 
         def gate_chunk(half, gate):
             cols = slice(half * N_TILE, (half + 1) * N_TILE)
-            gate_cols = slice(gate * HID + half * N_TILE, gate * HID + (half + 1) * N_TILE)
             accs = [psum.tile([P, N_TILE], F32, name="gate_acc_%d" % bt, tag="bank") for bt in range(BT)]
             for w, g in half_passes:
-                first = (FIRST_IH, FIRST_HH)[w] + 4 * g
                 for bt in range(BT):
                     mx_pass(
                         accs[bt][:], gate_acts[(w, g)], bt,
-                        gate_words[(w, half, gate)][:, g, :], gate_planes[first:P, gate_cols],
+                        gate_words[(w, half, gate)][:, g, :], gate_planes[(w, g)][4 * gate : P, cols],
                         (w, g) == half_passes[0], (w, g) == half_passes[-1],
                     )
             for bt in range(BT):

@@ -295,7 +295,6 @@ def tile_network_pb_kernel(
                     wm_words[:, g, :], wm_planes[4 * g : P, :], g == 0, g == HALVES - 1,
                 )
 
-        row_max = keep.tile([P, BT], F32, name="row_max")
         neg_max = keep.tile([P, BT], F32, name="neg_max")
         sum_exp = keep.tile([P, BT], F32, name="sum_exp")
         log_sum = keep.tile([P, BT], F32, name="log_sum")
@@ -303,8 +302,9 @@ def tile_network_pb_kernel(
         for bt in range(BT):
             nc.vector.tensor_tensor(out=motors[bt][:], in0=motor_acc[bt][:], in1=bm_spread[:], op=ALU.add)
         for bt in range(BT):
-            nc.vector.tensor_reduce(out=row_max[:, bt : bt + 1], in_=motors[bt][:], axis=AXIS.X, op=ALU.max)
-            nc.vector.tensor_scalar_mul(out=neg_max[:, bt : bt + 1], in0=row_max[:, bt : bt + 1], scalar1=-1.0)
+            nc.vector.tensor_reduce(
+                out=neg_max[:, bt : bt + 1], in_=motors[bt][:], axis=AXIS.X, op=ALU.max, negate=True
+            )
         for bt in range(BT):
             exps = keep.tile([P, MOTORS], F32, name="exps_%d" % bt)
             nc.scalar.activation(
@@ -312,11 +312,13 @@ def tile_network_pb_kernel(
                 bias=neg_max[:, bt : bt + 1], scale=1.0, accum_out=sum_exp[:, bt : bt + 1],
             )
         nc.scalar.activation(out=log_sum[:], in_=sum_exp[:], func=ACT.Ln)
-        for bt in range(BT):
-            preds = keep.tile([P, MOTORS], F32, name="preds_%d" % bt)
-            nc.vector.tensor_scalar(
-                out=preds[:], in0=motors[bt][:],
-                scalar1=row_max[:, bt : bt + 1], scalar2=log_sum[:, bt : bt + 1],
-                op0=ALU.subtract, op1=ALU.subtract,
-            )
-            nc.sync.dma_start(out=out_0[bt * P : (bt + 1) * P, :], in_=preds[:])
+        preds = [keep.tile([P, MOTORS], F32, name="preds_%d" % bt) for bt in range(BT)]
+        nc.vector.tensor_scalar(
+            out=preds[0][:], in0=motors[0][:],
+            scalar1=neg_max[:, 0:1], scalar2=log_sum[:, 0:1], op0=ALU.add, op1=ALU.subtract,
+        )
+        nc.sync.dma_start(out=out_0[0:P, :], in_=preds[0][:])
+        shift = keep.tile([P, 1], F32, name="shift")
+        nc.scalar.activation(out=shift[:], in_=log_sum[:, 1:2], func=ACT.Identity, bias=neg_max[:, 1:2], scale=-1.0)
+        nc.scalar.activation(out=preds[1][:], in_=motors[1][:], func=ACT.Identity, bias=shift[:], scale=1.0)
+        nc.scalar.dma_start(out=out_0[P : 2 * P, :], in_=preds[1][:])

@@ -118,22 +118,21 @@ def tile_network_pb_kernel(
                 nc.sync.dma_start(out=chunk[:].bitcast(I32), in_=packed_words(words)[:, :, col0 : col0 + N_TILE])
                 gate_words[(w, half, gate)] = chunk
 
+        y2_rows = load_rows(y2, HID, "y2_rows")
         for row0, vector in ((BIAS_ROW_IH, bih3), (BIAS_ROW_HH, bhh3), (BIAS_ROW_D, bd), (BIAS_ROW_M, bm)):
             load_bias(row0, vector)
-        y2_rows = load_rows(y2, HID, "y2_rows")
         h3_rows = load_rows(h3, HID, "h3_rows")
+        x_rows = load_rows(x, S_IN, "x_rows")
         for w in range(2):
             for g in range(2):
                 load_gate_scales(w, g)
-        x_rows = load_rows(x, S_IN, "x_rows")
         wd_words = keep.tile([P, 1, HID], U32, name="wd_words", align_bytes=64)
         nc.sync.dma_start(out=wd_words[:].bitcast(I32), in_=packed_words(Wd_words))
         load_scales(wd_planes, 0, Wd_scales)
         c3_rows = load_rows(c3, HID, "c3_rows")
         for half, gate in GATE_CHUNKS:
             load_gate_chunk(half, gate)
-            if (half, gate) == (1, GATE_I):
-                load_scales(wm_planes, 0, Wm_scales)
+        load_scales(wm_planes, 0, Wm_scales)
         wm_words = keep.tile([P, 2, MOTORS], U32, name="wm_words", align_bytes=64)
         nc.sync.dma_start(out=wm_words[:].bitcast(I32), in_=packed_words(Wm_words))
 

@@ -249,16 +249,23 @@ def tile_network_pb_kernel(
                     nc.scalar.activation(out=tanh_c[bt][:], in_=new_c[:], func=ACT.Tanh)
                     nc.sync.dma_start(out=out_2[bt * P : (bt + 1) * P, cols], in_=new_c[:])
 
-        def hidden_output(half, engine):
-            cols = slice(half * N_TILE, (half + 1) * N_TILE)
-            y3 = {}
+        y3 = {}
+
+        def hidden_y3(half, engine):
             for bt in range(BT):
-                y3[bt] = keep.tile([P, N_TILE], F32, name="y3_%d_%d" % (bt, half))
-                engine.tensor_tensor(out=y3[bt][:], in0=value[(GATE_O, bt)][:], in1=tanh_c[bt][:], op=ALU.mult)
+                y3[(bt, half)] = keep.tile([P, N_TILE], F32, name="y3_%d_%d" % (bt, half))
+                engine.tensor_tensor(
+                    out=y3[(bt, half)][:], in0=value[(GATE_O, bt)][:], in1=tanh_c[bt][:], op=ALU.mult
+                )
+
+        def hidden_mid(half, engine):
+            cols = slice(half * N_TILE, (half + 1) * N_TILE)
             for bt in range(BT):
                 mid[(bt, half)] = keep.tile([P, N_TILE], BF16, name="mid_%d_%d" % (bt, half))
-                engine.tensor_tensor(out=mid[(bt, half)][:], in0=y3[bt][:], in1=skip[(bt, half)][:], op=ALU.add)
-                nc.sync.dma_start(out=out_1[bt * P : (bt + 1) * P, cols], in_=y3[bt][:])
+                engine.tensor_tensor(
+                    out=mid[(bt, half)][:], in0=y3[(bt, half)][:], in1=skip[(bt, half)][:], op=ALU.add
+                )
+                nc.sync.dma_start(out=out_1[bt * P : (bt + 1) * P, cols], in_=y3[(bt, half)][:])
 
         mid_act = {}
 
@@ -278,9 +285,12 @@ def tile_network_pb_kernel(
 
         for half, gate in GATE_CHUNKS:
             gate_chunk(half, gate)
+            if (half, gate) == (0, GATE_O):
+                hidden_y3(0, nc.gpsimd)
             if (half, gate) == (1, GATE_F):
-                hidden_output(0, nc.gpsimd)
-        hidden_output(1, nc.vector)
+                hidden_mid(0, nc.gpsimd)
+        hidden_y3(1, nc.vector)
+        hidden_mid(1, nc.vector)
         bm_spread = spread_bias(ident_bf16[:, BIAS_ROW_M : BIAS_ROW_M + 1], False, "bm_spread")
 
         for half in range(HALVES):

@@ -114,9 +114,18 @@ def tile_network_pb_kernel(
         def load_gate_chunk(half, gate):
             col0 = gate * HID + half * N_TILE
             for w, words in enumerate((Wih3_words, Whh3_words)):
-                chunk = keep.tile([P, 2, N_TILE], U32, name="gate_words_%d_%d_%d" % (w, half, gate), align_bytes=64)
-                nc.sync.dma_start(out=chunk[:].bitcast(I32), in_=packed_words(words)[:, :, col0 : col0 + N_TILE])
-                gate_words[(w, half, gate)] = chunk
+                source = packed_words(words)[:, :, col0 : col0 + N_TILE]
+                name = "gate_words_%d_%d_%d" % (w, half, gate)
+                if w == 1 and (half, gate) in GATE_CHUNKS[-2:]:
+                    for g in range(2):
+                        piece = keep.tile([P, 1, N_TILE], U32, name="%s_%d" % (name, g), align_bytes=64)
+                        nc.sync.dma_start(out=piece[:].bitcast(I32), in_=source[:, g : g + 1, :])
+                        gate_words[(w, half, gate, g)] = piece[:, 0, :]
+                else:
+                    chunk = keep.tile([P, 2, N_TILE], U32, name=name, align_bytes=64)
+                    nc.sync.dma_start(out=chunk[:].bitcast(I32), in_=source)
+                    for g in range(2):
+                        gate_words[(w, half, gate, g)] = chunk[:, g, :]
 
         y2_rows = load_rows(y2, HID, "y2_rows")
         for row0, vector in ((BIAS_ROW_IH, bih3), (BIAS_ROW_HH, bhh3), (BIAS_ROW_D, bd), (BIAS_ROW_M, bm)):
@@ -223,7 +232,7 @@ def tile_network_pb_kernel(
                 for bt in range(BT):
                     mx_pass(
                         accs[bt][:], gate_acts[(w, g)], bt,
-                        gate_words[(w, half, gate)][:, g, :], gate_planes[(w, g)][4 * gate : P, cols],
+                        gate_words[(w, half, gate, g)], gate_planes[(w, g)][4 * gate : P, cols],
                         (w, g) == half_passes[0], (w, g) == half_passes[-1],
                     )
             for bt in range(BT):

@@ -83,9 +83,12 @@ def tile_network_pb_kernel(
         table_warm = keep.tile([P, 1], F32, name="table_warm")
         nc.scalar.activation(out=table_warm[:], in_=zero_col[:], func=ACT.Sigmoid)
 
+        def by_partition(dram):
+            return dram.rearrange("(p bt) n -> p bt n", bt=BT)
+
         def load_rows(src, width, name):
             rows = keep.tile([P, BT, width], BF16, name=name)
-            nc.sync.dma_start(out=rows[:], in_=src.rearrange("(bt p) k -> p bt k", p=P))
+            nc.sync.dma_start(out=rows[:], in_=by_partition(src))
             return rows
 
         def load_scales(plane_tile, first, scales):
@@ -256,7 +259,7 @@ def tile_network_pb_kernel(
                     )
                     tanh_c[bt] = keep.tile([P, N_TILE], F32, name="tanh_c_%d" % bt)
                     nc.scalar.activation(out=tanh_c[bt][:], in_=new_c[:], func=ACT.Tanh)
-                    nc.sync.dma_start(out=out_2[bt * P : (bt + 1) * P, cols], in_=new_c[:])
+                    nc.sync.dma_start(out=by_partition(out_2)[:, bt, cols], in_=new_c[:])
 
         y3 = {}
 
@@ -274,7 +277,7 @@ def tile_network_pb_kernel(
                 engine.tensor_tensor(
                     out=mid[(bt, half)][:], in0=y3[(bt, half)][:], in1=skip[(bt, half)][:], op=ALU.add
                 )
-                nc.sync.dma_start(out=out_1[bt * P : (bt + 1) * P, cols], in_=y3[(bt, half)][:])
+                nc.sync.dma_start(out=by_partition(out_1)[:, bt, cols], in_=y3[(bt, half)][:])
 
         mid_act = {}
 
@@ -335,8 +338,8 @@ def tile_network_pb_kernel(
             out=preds[0][:], in0=motors[0][:],
             scalar1=neg_max[:, 0:1], scalar2=log_sum[:, 0:1], op0=ALU.add, op1=ALU.subtract,
         )
-        nc.sync.dma_start(out=out_0[0:P, :], in_=preds[0][:])
+        nc.sync.dma_start(out=by_partition(out_0)[:, 0, :], in_=preds[0][:])
         shift = keep.tile([P, 1], F32, name="shift")
         nc.scalar.activation(out=shift[:], in_=log_sum[:, 1:2], func=ACT.Identity, bias=neg_max[:, 1:2], scale=-1.0)
         nc.scalar.activation(out=preds[1][:], in_=motors[1][:], func=ACT.Identity, bias=shift[:], scale=1.0)
-        nc.scalar.dma_start(out=out_0[P : 2 * P, :], in_=preds[1][:])
+        nc.scalar.dma_start(out=by_partition(out_0)[:, 1, :], in_=preds[1][:])

from contextlib import ExitStack

import concourse.mybir as mybir
from concourse.masks import make_identity

F32 = mybir.dt.float32
BF16 = mybir.dt.bfloat16
I32 = mybir.dt.int32
U32 = mybir.dt.uint32
U8 = mybir.dt.uint8
FP8X4 = mybir.dt.float8_e4m3fn_x4
ALU = mybir.AluOpType
ACT = mybir.ActivationFunctionType
AXIS = mybir.AxisListType

P = 128
PACK = 4
K_PASS = P * PACK
N_TILE = 512
QUADS = 4

BATCH = 256
BT = BATCH // P
S_IN = 512
HID = 1024
MOTORS = 512
HALVES = HID // N_TILE
GATE_I, GATE_F, GATE_G, GATE_O = 0, 1, 2, 3
GATE_ORDER = (GATE_F, GATE_I, GATE_G, GATE_O)
GATE_CHUNKS = [(half, gate) for half in range(HALVES) for gate in GATE_ORDER]
GATE_COLS = 4 * HID
GATE_PIECES = GATE_COLS // N_TILE
BIAS_ROW_IH = 0
BIAS_ROW_HH = BIAS_ROW_IH + GATE_PIECES
BIAS_ROW_D = BIAS_ROW_HH + GATE_PIECES
BIAS_ROW_M = BIAS_ROW_D + HALVES

FLOPS = 2 * BATCH * (2 * HID * GATE_COLS + S_IN * HID + HID * MOTORS)


def packed_words(words):
    return words.rearrange("g p n t -> p g (n t)").bitcast(I32)


def tile_network_pb_kernel(
    tc, x, y2, h3, c3,
    Wih3_words, Wih3_scales, Whh3_words, Whh3_scales, bih3, bhh3,
    Wd_words, Wd_scales, bd, Wm_words, Wm_scales, bm,
    out_0, out_1, out_2,
):
    nc = tc.nc
    with ExitStack() as stack:
        keep = stack.enter_context(tc.tile_pool(name="keep", bufs=1))
        psum = stack.enter_context(tc.psum_pool(name="psum", bufs=8))
        stack.enter_context(tc.manual_schedule())

        bias_rows = keep.tile([P, N_TILE], BF16, name="bias_rows")
        nc.vector.memset(bias_rows[:].bitcast(I32), 0)
        zero_col = keep.tile([P, 1], F32, name="zero_col")
        nc.vector.memset(zero_col[:], 0.0)
        gate_planes = {}
        for w in range(2):
            for g in range(2):
                gate_planes[(w, g)] = keep.tile([P, HID], U8, name="gate_planes_%d_%d" % (w, g), align_bytes=64)
                nc.vector.memset(gate_planes[(w, g)][:].bitcast(I32), 0)
        wd_planes = keep.tile([P, HID], U8, name="wd_planes", align_bytes=64)
        wm_planes = keep.tile([P, MOTORS], U8, name="wm_planes", align_bytes=64)
        nc.vector.memset(wd_planes[:].bitcast(I32), 0)
        nc.vector.memset(wm_planes[:].bitcast(I32), 0)

        ident_bf16 = keep.tile([P, P], BF16, name="ident_bf16")
        make_identity(nc, ident_bf16[:])
        gate_pick = keep.tile([P, GATE_PIECES], BF16, name="gate_pick")
        nc.gpsimd.tensor_tensor(
            out=gate_pick[:],
            in0=ident_bf16[:, BIAS_ROW_IH : BIAS_ROW_IH + GATE_PIECES],
            in1=ident_bf16[:, BIAS_ROW_HH : BIAS_ROW_HH + GATE_PIECES],
            op=ALU.add,
        )
        ident_f32 = keep.tile([P, P], F32, name="ident_f32")
        make_identity(nc, ident_f32[:])

        table_warm = keep.tile([P, 1], F32, name="table_warm")
        nc.scalar.activation(out=table_warm[:], in_=zero_col[:], func=ACT.Sigmoid)

        def by_partition(dram):
            return dram.rearrange("(p bt) n -> p bt n", bt=BT)

        def load_rows(src, width, name):
            rows = keep.tile([P, BT, width], BF16, name=name)
            nc.sync.dma_start(out=rows[:], in_=by_partition(src))
            return rows

        def load_scales(plane_tile, first, scales):
            passes = scales.shape[0]
            for quad in range(QUADS):
                top = 32 * quad + first
                nc.sync.dma_start(
                    out=plane_tile[top : top + 4 * passes, :].bitcast(I32),
                    in_=scales[:, 4 * quad : 4 * quad + 4, :].bitcast(I32),
                )

        def load_gate_scales(w, g):
            scales = (Wih3_scales, Whh3_scales)[w]
            for quad in range(QUADS):
                nc.sync.dma_start(
                    out=gate_planes[(w, g)][32 * quad : 32 * quad + 16, :].bitcast(I32),
                    in_=scales[g, 4 * quad : 4 * quad + 4, :].rearrange("r (j c) -> j r c", j=4).bitcast(I32),
                )

        def load_bias(row0, vector):
            pieces = vector.rearrange("(r n) -> r n", n=N_TILE)
            nc.sync.dma_start(out=bias_rows[row0 : row0 + pieces.shape[0], :], in_=pieces)

        gate_words = {}

        def load_gate_chunk(half, gate):
            col0 = gate * HID + half * N_TILE
            for w, words in enumerate((Wih3_words, Whh3_words)):
                source = packed_words(words)[:, :, col0 : col0 + N_TILE]
                name = "gate_words_%d_%d_%d" % (w, half, gate)
                if w == 1 and (half, gate) in GATE_CHUNKS[-2:]:
                    for g in range(2):
                        piece = keep.tile([P, 1, N_TILE], U32, name="%s_%d" % (name, g), align_bytes=64)
                        nc.sync.dma_start(out=piece[:].bitcast(I32), in_=source[:, g : g + 1, :])
                        gate_words[(w, half, gate, g)] = piece[:, 0, :]
                else:
                    chunk = keep.tile([P, 2, N_TILE], U32, name=name, align_bytes=64)
                    nc.sync.dma_start(out=chunk[:].bitcast(I32), in_=source)
                    for g in range(2):
                        gate_words[(w, half, gate, g)] = chunk[:, g, :]

        y2_rows = load_rows(y2, HID, "y2_rows")
        for row0, vector in ((BIAS_ROW_IH, bih3), (BIAS_ROW_HH, bhh3), (BIAS_ROW_D, bd), (BIAS_ROW_M, bm)):
            load_bias(row0, vector)
        h3_rows = load_rows(h3, HID, "h3_rows")
        x_rows = load_rows(x, S_IN, "x_rows")
        for w in range(2):
            for g in range(2):
                load_gate_scales(w, g)
        wd_words = keep.tile([P, 1, HID], U32, name="wd_words", align_bytes=64)
        nc.sync.dma_start(out=wd_words[:].bitcast(I32), in_=packed_words(Wd_words))
        load_scales(wd_planes, 0, Wd_scales)
        c3_rows = load_rows(c3, HID, "c3_rows")
        for half, gate in GATE_CHUNKS:
            load_gate_chunk(half, gate)
        load_scales(wm_planes, 0, Wm_scales)
        wm_words = keep.tile([P, 2, MOTORS], U32, name="wm_words", align_bytes=64)
        nc.sync.dma_start(out=wm_words[:].bitcast(I32), in_=packed_words(Wm_words))

        def copy_out(on_vector, out, in_):
            if on_vector:
                nc.vector.tensor_copy(out=out, in_=in_)
            else:
                nc.scalar.copy(out=out, in_=in_)

        def quantise_rows(rows, g, on_vector, name):
            flipped = psum.tile([P, BT, 2, P], F32, name="flipped_" + name, tag="bank")
            for bt in range(BT):
                pairs = rows[:, bt, :].bitcast(F32)
                for u in range(2):
                    nc.tensor.transpose(
                        flipped[:, bt, u, :], pairs[:, 256 * g + u : 256 * (g + 1) : 2], ident_f32[:]
                    )
            grouped = keep.tile([P, BATCH * PACK], BF16, name="grouped_" + name, align_bytes=64)
            copy_out(
                on_vector,
                grouped[:].bitcast(F32).rearrange("p (bt b u) -> p bt b u", bt=BT, u=2),
                flipped[:].rearrange("p bt u b -> p bt b u"),
            )
            codes = keep.tile([P, BATCH], U32, name="codes_" + name, align_bytes=64)
            plane = keep.tile([P, BATCH], U8, name="plane_" + name, align_bytes=64)
            nc.vector.quantize_mx(out=codes[:].bitcast(FP8X4), scales=plane[:], in_=grouped[:])
            return codes, plane

        def mx_pass(acc, act, bt, words, plane, start, stop):
            codes, act_plane = act
            tile_cols = slice(bt * P, (bt + 1) * P)
            nc.tensor.matmul_mx(
                out=acc,
                lhsT=codes[:, tile_cols].bitcast(FP8X4),
                lhsT_scale=act_plane[:, tile_cols],
                rhs=words.bitcast(FP8X4),
                rhs_scale=plane,
                start=start,
                stop=stop,
            )

        def spread_bias(pick, on_vector, name):
            bank = psum.tile([P, N_TILE], F32, name="bank_" + name, tag="bank")
            nc.tensor.matmul(bank[:], lhsT=pick.to_broadcast([P, P]), rhs=bias_rows[:], start=True, stop=True)
            spread = keep.tile([P, N_TILE], F32, name=name)
            copy_out(on_vector, spread[:], bank[:])
            return spread

        gate_bias = {}

        def spread_gate_biases(half, on_vector):
            for gate in GATE_ORDER:
                piece = 2 * gate + half
                gate_bias[(half, gate)] = spread_bias(
                    gate_pick[:, piece : piece + 1], on_vector, "gate_bias_%d_%d" % (half, gate)
                )

        spread_gate_biases(0, True)
        gate_acts = {}
        for w, rows in enumerate((y2_rows, h3_rows)):
            for g in range(2):
                gate_acts[(w, g)] = quantise_rows(rows, g, False, "gate_%d_%d" % (w, g))
        bd_spread = [
            spread_bias(ident_bf16[:, BIAS_ROW_D + half : BIAS_ROW_D + half + 1], False, "bd_spread_%d" % half)
            for half in range(HALVES)
        ]
        x_act = quantise_rows(x_rows, 0, True, "x")
        spread_gate_biases(1, False)

        skip = {}
        for half in range(HALVES):
            cols = slice(half * N_TILE, (half + 1) * N_TILE)
            for bt in range(BT):
                skip_acc = psum.tile([P, N_TILE], F32, name="skip_acc", tag="bank")
                mx_pass(skip_acc[:], x_act, bt, wd_words[:, 0, cols], wd_planes[:, cols], True, True)
                skip[(bt, half)] = keep.tile([P, N_TILE], F32, name="skip_%d_%d" % (bt, half))
                nc.vector.tensor_tensor(out=skip[(bt, half)][:], in0=skip_acc[:], in1=bd_spread[half][:], op=ALU.add)

        value = {}
        tanh_c = {}
        mid = {}
        half_passes = [(w, g) for w in range(2) for g in range(2)]

        def gate_chunk(half, gate):
            cols = slice(half * N_TILE, (half + 1) * N_TILE)
            accs = [psum.tile([P, N_TILE], F32, name="gate_acc_%d" % bt, tag="bank") for bt in range(BT)]
            for w, g in half_passes:
                for bt in range(BT):
                    mx_pass(
                        accs[bt][:], gate_acts[(w, g)], bt,
                        gate_words[(w, half, gate, g)], gate_planes[(w, g)][4 * gate : P, cols],
                        (w, g) == half_passes[0], (w, g) == half_passes[-1],
                    )
            for bt in range(BT):
                out = keep.tile([P, N_TILE], F32, name="value_%d_%d" % (gate, bt))
                nc.vector.tensor_tensor(out=out[:], in0=accs[bt][:], in1=gate_bias[(half, gate)][:], op=ALU.add)
                nc.scalar.activation(out=out[:], in_=out[:], func=ACT.Tanh if gate == GATE_G else ACT.Sigmoid)
                value[(gate, bt)] = out

            if gate == GATE_F:
                for bt in range(BT):
                    kept = value[(GATE_F, bt)]
                    nc.gpsimd.tensor_tensor(out=kept[:], in0=kept[:], in1=c3_rows[:, bt, cols], op=ALU.mult)
            if gate == GATE_G:
                for bt in range(BT):
                    fresh = value[(GATE_G, bt)]
                    nc.vector.tensor_tensor(out=fresh[:], in0=fresh[:], in1=value[(GATE_I, bt)][:], op=ALU.mult)
                for bt in range(BT):
                    new_c = keep.tile([P, N_TILE], F32, name="new_c_%d_%d" % (bt, half))
                    nc.vector.tensor_tensor(
                        out=new_c[:], in0=value[(GATE_F, bt)][:], in1=value[(GATE_G, bt)][:], op=ALU.add
                    )
                    tanh_c[bt] = keep.tile([P, N_TILE], F32, name="tanh_c_%d" % bt)
                    nc.scalar.activation(out=tanh_c[bt][:], in_=new_c[:], func=ACT.Tanh)
                    nc.sync.dma_start(out=by_partition(out_2)[:, bt, cols], in_=new_c[:])

        y3 = {}

        def hidden_y3(half, engine):
            for bt in range(BT):
                y3[(bt, half)] = keep.tile([P, N_TILE], F32, name="y3_%d_%d" % (bt, half))
                engine.tensor_tensor(
                    out=y3[(bt, half)][:], in0=value[(GATE_O, bt)][:], in1=tanh_c[bt][:], op=ALU.mult
                )

        def hidden_mid(half, engine):
            cols = slice(half * N_TILE, (half + 1) * N_TILE)
            for bt in range(BT):
                mid[(bt, half)] = keep.tile([P, N_TILE], BF16, name="mid_%d_%d" % (bt, half))
                engine.tensor_tensor(
                    out=mid[(bt, half)][:], in0=y3[(bt, half)][:], in1=skip[(bt, half)][:], op=ALU.add
                )
                nc.sync.dma_start(out=by_partition(out_1)[:, bt, cols], in_=y3[(bt, half)][:])

        mid_act = {}

        def flip_mid(half):
            for bt in range(BT):
                flipped = psum.tile([P, PACK, P], BF16, name="flipped_mid", tag="bank")
                for t in range(PACK):
                    nc.tensor.transpose(flipped[:, t, :], mid[(bt, half)][:, t:N_TILE:PACK], ident_bf16[:])
                grouped = keep.tile([P, P * PACK], BF16, name="grouped_mid_%d_%d" % (bt, half), align_bytes=64)
                nc.scalar.copy(
                    out=grouped[:].rearrange("p (b t) -> p b t", t=PACK), in_=flipped[:].rearrange("p t b -> p b t")
                )
                codes = keep.tile([P, P], U32, name="codes_mid_%d_%d" % (bt, half), align_bytes=64)
                plane = keep.tile([P, P], U8, name="plane_mid_%d_%d" % (bt, half), align_bytes=64)
                nc.vector.quantize_mx(out=codes[:].bitcast(FP8X4), scales=plane[:], in_=grouped[:])
                mid_act[(bt, half)] = (codes, plane)

        for half, gate in GATE_CHUNKS:
            gate_chunk(half, gate)
            if (half, gate) == (0, GATE_O):
                hidden_y3(0, nc.gpsimd)
            if (half, gate) == (1, GATE_F):
                hidden_mid(0, nc.gpsimd)
        hidden_y3(1, nc.vector)
        hidden_mid(1, nc.vector)
        bm_spread = spread_bias(ident_bf16[:, BIAS_ROW_M : BIAS_ROW_M + 1], False, "bm_spread")

        for half in range(HALVES):
            flip_mid(half)
        nc.scalar.activation(out=table_warm[:], in_=zero_col[:], func=ACT.Exp)
        motor_acc = [psum.tile([P, MOTORS], F32, name="motor_acc_%d" % bt, tag="bank") for bt in range(BT)]
        for g in range(HALVES):
            for bt in range(BT):
                mx_pass(
                    motor_acc[bt][:], mid_act[(bt, g)], 0,
                    wm_words[:, g, :], wm_planes[4 * g : P, :], g == 0, g == HALVES - 1,
                )

        neg_max = keep.tile([P, BT], F32, name="neg_max")
        sum_exp = keep.tile([P, BT], F32, name="sum_exp")
        log_sum = keep.tile([P, BT], F32, name="log_sum")
        motors = [keep.tile([P, MOTORS], F32, name="motors_%d" % bt) for bt in range(BT)]
        for bt in range(BT):
            nc.vector.tensor_tensor(out=motors[bt][:], in0=motor_acc[bt][:], in1=bm_spread[:], op=ALU.add)
        for bt in range(BT):
            nc.vector.tensor_reduce(
                out=neg_max[:, bt : bt + 1], in_=motors[bt][:], axis=AXIS.X, op=ALU.max, negate=True
            )
        for bt in range(BT):
            exps = keep.tile([P, MOTORS], F32, name="exps_%d" % bt)
            nc.scalar.activation(
                out=exps[:], in_=motors[bt][:], func=ACT.Exp,
                bias=neg_max[:, bt : bt + 1], scale=1.0, accum_out=sum_exp[:, bt : bt + 1],
            )
        nc.scalar.activation(out=log_sum[:], in_=sum_exp[:], func=ACT.Ln)
        preds = [keep.tile([P, MOTORS], F32, name="preds_%d" % bt) for bt in range(BT)]
        nc.vector.tensor_scalar(
            out=preds[0][:], in0=motors[0][:],
            scalar1=neg_max[:, 0:1], scalar2=log_sum[:, 0:1], op0=ALU.add, op1=ALU.subtract,
        )
        nc.sync.dma_start(out=by_partition(out_0)[:, 0, :], in_=preds[0][:])
        shift = keep.tile([P, 1], F32, name="shift")
        nc.scalar.activation(out=shift[:], in_=log_sum[:, 1:2], func=ACT.Identity, bias=neg_max[:, 1:2], scale=-1.0)
        nc.scalar.activation(out=preds[1][:], in_=motors[1][:], func=ACT.Identity, bias=shift[:], scale=1.0)
        nc.scalar.dma_start(out=by_partition(out_0)[:, 1, :], in_=preds[1][:])
